import numpy as np
import ml_dtypes


def mxq(x, axis, fmt="e4m3"):
    dtype, down = {"e4m3": (ml_dtypes.float8_e4m3fn, 7), "e5m2": (ml_dtypes.float8_e5m2, 14)}[fmt]
    v = np.moveaxis(np.asarray(x, np.float32).astype(ml_dtypes.bfloat16).astype(np.float64), axis, -1)
    blocks = v.reshape(v.shape[:-1] + (-1, 32))
    amax = np.abs(blocks).max(-1, keepdims=True)
    byte = np.maximum(np.where(amax > 0, np.frexp(amax)[1] - 1 + 127, 0) - down, 1)
    scale = np.exp2(byte - 127.0)
    codes = (blocks / scale).astype(np.float32).astype(dtype).astype(np.float64)
    return np.moveaxis((codes * scale).reshape(v.shape), -1, axis)


WIDE = False


def mx_kscale(k):
    if not WIDE:
        return np.ones(k)
    levels = np.array([30, -30])
    if k % 512:
        return np.exp2(np.random.permutation(np.resize(levels, k // 32))).repeat(32)
    a = np.empty((k // 512, 16))
    for p in range(k // 512):
        a[p, :8] = np.random.permutation(np.resize(levels, 8))
        for g in range(8):
            far = levels[np.abs(levels - a[p, g]) >= 10]
            a[p, g + 8] = far[np.random.randint(len(far))]
    return np.exp2(a.ravel()).repeat(32)


BF16 = ml_dtypes.bfloat16


def bf(x):
    return np.asarray(x, np.float32).astype(BF16)


def f64(x):
    return np.asarray(x).astype(np.float64)


E2M1 = np.array([0.0, 0.5, 1.0, 1.5, 2.0, 3.0, 4.0, 6.0, -0.0, -0.5, -1.0, -1.5, -2.0, -3.0, -4.0, -6.0])


def pack_weight(w, fmt):
    k, n = w.shape
    w = f64(bf(w)).reshape(k // 32, 32, n)
    amax = np.abs(w).max(1)
    if fmt == "e4m3":
        byte = np.frexp(amax)[1] - 1 + 127 - 7
    else:
        mant, ex = np.frexp(amax / 6.0)
        byte = np.where(mant > 0.5, ex, ex - 1) + 127
    byte = np.clip(np.where(amax > 0, byte, 1), 1, 254)
    scaled = (w * np.exp2(127.0 - byte)[:, None, :]).reshape(k, n).astype(np.float32)
    by_word = np.ascontiguousarray(scaled.reshape(k // 512, 128, 4, n).transpose(0, 1, 3, 2))
    if fmt == "e4m3":
        words = by_word.astype(ml_dtypes.float8_e4m3fn).view(np.uint8)
    else:
        c = by_word.astype(ml_dtypes.float4_e2m1fn).view(np.uint8) & 0xF
        words = c[..., 0::2] | (c[..., 1::2] << 4)
    return np.ascontiguousarray(words), np.ascontiguousarray(byte.astype(np.uint8).reshape(k // 512, 16, n))


def unpack_weight(words, scales, fmt):
    g, p, n, _ = words.shape
    if fmt == "e4m3":
        vals = np.ascontiguousarray(words).view(ml_dtypes.float8_e4m3fn).astype(np.float64)
    else:
        nib = np.empty((g, p, n, 4), np.uint8)
        nib[..., 0::2] = words & 0xF
        nib[..., 1::2] = words >> 4
        vals = E2M1[nib]
    vals = vals * np.repeat(np.exp2(scales.astype(np.float64) - 127.0), 8, axis=1)[..., None]
    return vals.transpose(0, 1, 3, 2).reshape(g * 512, n)

def pack4(w):
    words, scales = pack_weight(w, "e2m1")
    return words.reshape(words.shape[0], 128, -1), scales


def unpack4(words, scales):
    return unpack_weight(words.reshape(words.shape[0], 128, -1, 2), scales, "e2m1")


B, S, HIDDEN, H, HKV, D = 1, 512, 2048, 16, 4, 128
THETA = 10000.0
QS, KVS = H * D, HKV * D
HALF = D // 2


def rope(x):
    freqs = 1.0 / THETA ** (np.arange(0, D, 2) / D)
    ang = np.arange(S)[:, None] * freqs[None, :]
    cos = np.cos(ang)[None, :, None, :]
    sin = np.sin(ang)[None, :, None, :]
    x1, x2 = x[..., :HALF], x[..., HALF:]
    return np.concatenate([x1 * cos - x2 * sin, x1 * sin + x2 * cos], axis=-1)


def setup_inputs():
    s = mx_kscale(HIDDEN)
    hidden_states = bf(np.random.standard_normal((B, S, HIDDEN)) * s)
    w = np.random.standard_normal((QS + 2 * KVS, HIDDEN)) * 1.2 / np.sqrt(HIDDEN) / s
    words, scales = pack4(np.ascontiguousarray(w.T))
    return {"hidden_states": hidden_states,
            "w_qkv_words": words,
            "w_qkv_scales": scales}


def reference(hidden_states, w_qkv_words, w_qkv_scales):
    qkv = mxq(f64(hidden_states), 2, "e5m2") @ unpack4(w_qkv_words, w_qkv_scales)
    xq = qkv[..., :QS].reshape(B, S, H, D)
    xk = qkv[..., QS:QS + KVS].reshape(B, S, HKV, D)
    xv = qkv[..., QS + KVS:].reshape(B, S, HKV, D)
    return rope(xq), rope(xk), xv

@@ -1,0 +1,191 @@
+import math
+from contextlib import ExitStack
+
+import concourse.mybir as mybir
+from concourse.masks import make_identity
+
+F32 = mybir.dt.float32
+BF16 = mybir.dt.bfloat16
+I32 = mybir.dt.int32
+U32 = mybir.dt.uint32
+U8 = mybir.dt.uint8
+E5M2X4 = mybir.dt.float8_e5m2_x4
+E2M1X4 = mybir.dt.float4_e2m1fn_x4
+ALU = mybir.AluOpType
+ACT = mybir.ActivationFunctionType
+
+P = 128
+TOKENS, HIDDEN, OUT_COLS = 512, 2048, 3072
+HEAD, HALF = 128, 64
+THETA = 10000.0
+PASSES = HIDDEN // 512
+TILES = TOKENS // P
+BLOCK = 512
+BLOCKS = OUT_COLS // BLOCK
+HEADS_PER_BLOCK = BLOCK // HEAD
+Q_BLOCKS = 4
+K_BLOCK, V_BLOCK = 4, 5
+
+FLOPS = 2 * TOKENS * HIDDEN * OUT_COLS
+
+
+def tile_gemmaattention_pa_kernel(tc, hidden_states, w_qkv_words, w_qkv_scales, out_0, out_1, out_2):
+    nc = tc.nc
+    x_hbm = hidden_states.rearrange("b s k -> (b s) k")
+    q_hbm = out_0.rearrange("b s h d -> (b s) (h d)")
+    k_hbm = out_1.rearrange("b s h d -> (b s) (h d)")
+    v_hbm = out_2.rearrange("b s h d -> (b s) (h d)")
+    words_hbm = w_qkv_words.rearrange("g p c -> p g c")
+    scales_hbm = w_qkv_scales.rearrange("g (quad r) n -> r quad g n", r=4)
+
+    with ExitStack() as ctx:
+        keep = ctx.enter_context(tc.tile_pool(name="keep", bufs=1))
+        work = ctx.enter_context(tc.tile_pool(name="work", bufs=3))
+        psum = ctx.enter_context(tc.psum_pool(name="psum", bufs=8))
+        ctx.enter_context(tc.manual_schedule())
+
+        x_halves = [[keep.tile([P, HIDDEN // 2], BF16, name="x_%d_%d" % (t, b), align_bytes=64) for b in range(2)]
+                    for t in range(1)]
+        x_rest = [keep.tile([P, HIDDEN], BF16, name="x_%d" % t, align_bytes=64) for t in range(1, TILES)]
+        codes = [[keep.tile([P, 2, P], U32, name="codes_%d_%d" % (t, b), align_bytes=64) for b in range(2)]
+                 for t in range(TILES)]
+        x_scales = [[keep.tile([P, 2, P], U8, name="xscales_%d_%d" % (t, b), align_bytes=64) for b in range(2)]
+                    for t in range(TILES)]
+        plane_first = keep.tile([P, PASSES, BLOCK], U8, name="plane_first", align_bytes=64)
+        plane_rest = keep.tile([P, PASSES, OUT_COLS - BLOCK], U8, name="plane_rest", align_bytes=64)
+        w_first = [keep.tile([P, 2, 2 * BLOCK], U8, name="w_first_%d" % b, align_bytes=64) for b in range(2)]
+        w_groups = [(1, 2), (2, 4), (4, 6)]
+        w_rest = [keep.tile([P, PASSES, 2 * BLOCK * (hi - lo)], U8, name="w_%d" % lo, align_bytes=64)
+                  for lo, hi in w_groups]
+        identity = keep.tile([P, P], F32, name="identity")
+        position = keep.tile([P, TILES], I32, name="position")
+        turns = keep.tile([P, TILES, 2, HALF], F32, name="turns")
+        whole = keep.tile([P, TILES, 2, HALF], I32, name="whole")
+        frac = keep.tile([P, TILES, 2, HALF], F32, name="frac")
+        table = keep.tile([P, TILES, 4, HALF], F32, name="table")
+
+        nc.gpsimd.iota(position[:], pattern=[[P, TILES]], base=0, channel_multiplier=1)
+        make_identity(nc, identity[:])
+
+        fills = [plane_first[:].rearrange("p g n -> p (g n)")] + [plane_rest[:, g, :] for g in range(PASSES)]
+        nc.vector.memset(fills[0].bitcast(I32), 0)
+        nc.vector.tensor_scalar(out=turns[:, :, 1, 0], in0=position[:], scalar1=1.0 / (2.0 * math.pi), scalar2=None,
+                                op0=ALU.mult)
+        for step in range(6):
+            n = 1 << step
+            nc.vector.tensor_scalar(out=turns[:, :, 1, n:2 * n], in0=turns[:, :, 1, 0:n],
+                                    scalar1=THETA ** (-n / HALF), scalar2=None, op0=ALU.mult)
+        nc.vector.tensor_scalar(out=turns[:, :, 0, :], in0=turns[:, :, 1, :], scalar1=0.25, scalar2=None, op0=ALU.add)
+        nc.vector.memset(fills[1].bitcast(I32), 0)
+        nc.vector.tensor_copy(out=whole[:], in_=turns[:])
+        nc.vector.memset(fills[2].bitcast(I32), 0)
+        nc.vector.tensor_tensor(out=frac[:], in0=turns[:], in1=whole[:], op=ALU.subtract)
+        nc.vector.memset(fills[3].bitcast(I32), 0)
+        nc.vector.memset(fills[4].bitcast(I32), 0)
+        nc.scalar.activation(out=table[:, :, 0:2, :], in_=frac[:], func=ACT.Sin, scale=2.0 * math.pi)
+        nc.scalar.activation(out=table[:, :, 2, :], in_=frac[:, :, 1, :], func=ACT.Sin, scale=-2.0 * math.pi)
+        nc.vector.tensor_copy(out=table[:, :, 3, :], in_=table[:, :, 0, :])
+
+        for b in range(2):
+            nc.sync.dma_start(out=x_halves[0][b][:], in_=x_hbm[0:P, b * 1024:(b + 1) * 1024])
+        for t in range(1, TILES):
+            nc.sync.dma_start(out=x_rest[t - 1][:], in_=x_hbm[t * P:(t + 1) * P, :])
+
+        def load_scales(plane, lo, hi):
+            for r in range(4):
+                nc.sync.dma_start(out=plane[r:P:32, :, :].bitcast(I32), in_=scales_hbm[r, :, :, lo:hi].bitcast(I32))
+
+        load_scales(plane_first, 0, BLOCK)
+        for b in range(2):
+            nc.sync.dma_start(out=w_first[b][:].bitcast(I32),
+                              in_=words_hbm[:, 2 * b:2 * b + 2, 0:2 * BLOCK].bitcast(I32))
+        load_scales(plane_rest, BLOCK, OUT_COLS)
+        for w_tile, (lo, hi) in zip(w_rest, w_groups):
+            nc.sync.dma_start(out=w_tile[:].bitcast(I32),
+                              in_=words_hbm[:, :, 2 * BLOCK * lo:2 * BLOCK * hi].bitcast(I32))
+
+        def weight_operand(j, g, lo, hi):
+            if j == 0:
+                return w_first[g // 2][:, g % 2, 2 * lo:2 * hi], plane_first[:, g, lo:hi]
+            index = [i for i, (a, b) in enumerate(w_groups) if a <= j < b][0]
+            base = (j - w_groups[index][0]) * BLOCK
+            plane_base = (j - 1) * BLOCK
+            return (w_rest[index][:, g, 2 * (base + lo):2 * (base + hi)],
+                    plane_rest[:, g, plane_base + lo:plane_base + hi])
+
+        for t in range(TILES):
+            for b in range(2):
+                if t == 0:
+                    x_words = x_halves[0][b][:].bitcast(F32)
+                else:
+                    x_words = x_rest[t - 1][:, b * 1024:(b + 1) * 1024].bitcast(F32)
+                flipped = psum.tile([P, 2, 2, P], F32, name="flipped", tag="bank")
+                for g in range(2):
+                    for u in range(2):
+                        nc.tensor.transpose(flipped[:, g, u, :], x_words[:, 256 * g + u:256 * (g + 1):2], identity[:])
+                grouped = work.tile([P, 2, P, 2], F32, name="grouped", align_bytes=64)
+                nc.scalar.copy(out=grouped[:], in_=flipped[:].rearrange("p g u r -> p g r u"))
+                nc.vector.quantize_mx(out=codes[t][b][:].rearrange("p g r -> p (g r)").bitcast(E5M2X4),
+                                      scales=x_scales[t][b][:].rearrange("p g r -> p (g r)"),
+                                      in_=grouped[:].rearrange("p g r u -> p (g r u)").bitcast(BF16))
+
+        def project(t, j, lo, hi):
+            acc = psum.tile([P, BLOCK], F32, name="acc", tag="bank")
+            for g in range(PASSES):
+                w_words, w_scales = weight_operand(j, g, lo, hi)
+                nc.tensor.matmul_mx(out=acc[:, 0:hi - lo], lhsT=codes[t][g // 2][:, g % 2, :].bitcast(E5M2X4),
+                                    lhsT_scale=x_scales[t][g // 2][:, g % 2, :],
+                                    rhs=w_words.bitcast(E2M1X4), rhs_scale=w_scales,
+                                    start=(g == 0), stop=(g == PASSES - 1))
+            return acc
+
+        def rotate_products(t, acc, products):
+            halves = acc[:].rearrange("p (hh one i) -> p hh one i", one=1, i=HALF)
+            nc.vector.tensor_tensor(
+                out=products.rearrange("p h src n -> p (h src n)").rearrange("p (hh dst i) -> p hh dst i", dst=2, i=HALF),
+                in0=halves.to_broadcast([P, 2 * HEADS_PER_BLOCK, 2, HALF]),
+                in1=table[:, t:t + 1, :, :].rearrange("p one q i -> p one (q i)").to_broadcast([P, HEADS_PER_BLOCK, 4 * HALF]),
+                op=ALU.mult)
+
+        def add_and_store(engine, products, dest, tiles):
+            count = len(tiles)
+            rotated = work.tile([P, 2, HEADS_PER_BLOCK, HEAD], F32, name="rotated", bufs=6)
+            engine.tensor_tensor(out=rotated[:, 0:count, :, :].rearrange("p s h n -> p (s h) n"),
+                                 in0=products[:, 0:count, :, 0, :].rearrange("p s h n -> p (s h) n"),
+                                 in1=products[:, 0:count, :, 1, :].rearrange("p s h n -> p (s h) n"), op=ALU.add)
+            rows = dest[tiles[0] * P:(tiles[-1] + 1) * P, :].rearrange("(s p) n -> p s n", p=P)
+            nc.sync.dma_start(out=rows, in_=rotated[:, 0:count, :, :].rearrange("p s h n -> p s (h n)"))
+
+        late = []
+        for j in range(K_BLOCK + 1):
+            dest = q_hbm[:, j * BLOCK:(j + 1) * BLOCK] if j < Q_BLOCKS else k_hbm
+            if j == 0:
+                groups = [[0], [1], [2, 3]]
+            elif j == K_BLOCK:
+                groups = [[0], [1], [2], [3]]
+            else:
+                groups = [[0, 1], [2, 3]]
+            for tiles in groups:
+                products = work.tile([P, 2, HEADS_PER_BLOCK, 2, HEAD], F32, name="products", bufs=4)
+                for s, t in enumerate(tiles):
+                    acc = project(t, j, 0, BLOCK)
+                    rotate_products(t, acc, products[:, s, :, :, :])
+                if j == K_BLOCK and tiles[0] >= 1:
+                    late.append((products, dest, tiles))
+                else:
+                    add_and_store(nc.gpsimd, products, dest, tiles)
+
+        def store_values(t, lo, hi):
+            acc = project(t, V_BLOCK, lo, hi)
+            values = work.tile([P, BLOCK], F32, name="values", bufs=5)
+            nc.scalar.copy(out=values[:, 0:hi - lo], in_=acc[:, 0:hi - lo])
+            nc.scalar.dma_start(out=v_hbm[t * P:(t + 1) * P, lo:hi], in_=values[:, 0:hi - lo])
+
+        store_values(0, 0, BLOCK)
+        add_and_store(nc.vector, *late[0])
+        store_values(1, 0, BLOCK)
+        add_and_store(nc.vector, *late[1])
+        add_and_store(nc.vector, *late[2])
+        store_values(2, 0, BLOCK)
+        store_values(3, 0, BLOCK // 2)
+        store_values(3, BLOCK // 2, BLOCK)

@@ -25,6 +25,7 @@ BLOCKS = OUT_COLS // BLOCK
 HEADS_PER_BLOCK = BLOCK // HEAD
 Q_BLOCKS = 4
 K_BLOCK, V_BLOCK = 4, 5
+RADIX = 8
 
 FLOPS = 2 * TOKENS * HIDDEN * OUT_COLS
 
@@ -44,22 +45,22 @@ def tile_gemmaattention_pa_kernel(tc, hidden_states, w_qkv_words, w_qkv_scales, 
         psum = ctx.enter_context(tc.psum_pool(name="psum", bufs=8))
         ctx.enter_context(tc.manual_schedule())
 
-        x_halves = [[keep.tile([P, HIDDEN // 2], BF16, name="x_%d_%d" % (t, b), align_bytes=64) for b in range(2)]
-                    for t in range(1)]
+        x_first = [keep.tile([P, HIDDEN // 2], BF16, name="x_0_%d" % b, align_bytes=64) for b in range(2)]
         x_rest = [keep.tile([P, HIDDEN], BF16, name="x_%d" % t, align_bytes=64) for t in range(1, TILES)]
         codes = [[keep.tile([P, 2, P], U32, name="codes_%d_%d" % (t, b), align_bytes=64) for b in range(2)]
                  for t in range(TILES)]
         x_scales = [[keep.tile([P, 2, P], U8, name="xscales_%d_%d" % (t, b), align_bytes=64) for b in range(2)]
                     for t in range(TILES)]
-        plane_first = keep.tile([P, PASSES, BLOCK], U8, name="plane_first", align_bytes=64)
-        plane_rest = keep.tile([P, PASSES, OUT_COLS - BLOCK], U8, name="plane_rest", align_bytes=64)
+        plane_groups = [(0, 1), (1, 2), (2, 6)]
+        planes = [keep.tile([P, PASSES, BLOCK * (hi - lo)], U8, name="plane_%d" % lo, align_bytes=64)
+                  for lo, hi in plane_groups]
         w_first = [keep.tile([P, 2, 2 * BLOCK], U8, name="w_first_%d" % b, align_bytes=64) for b in range(2)]
         w_groups = [(1, 2), (2, 4), (4, 6)]
         w_rest = [keep.tile([P, PASSES, 2 * BLOCK * (hi - lo)], U8, name="w_%d" % lo, align_bytes=64)
                   for lo, hi in w_groups]
         identity = keep.tile([P, P], F32, name="identity")
         position = keep.tile([P, TILES], I32, name="position")
-        turns = keep.tile([P, TILES, 2, HALF], F32, name="turns")
+        turns = keep.tile([P, TILES, HALF], F32, name="turns")
         whole = keep.tile([P, TILES, 2, HALF], I32, name="whole")
         frac = keep.tile([P, TILES, 2, HALF], F32, name="frac")
         table = keep.tile([P, TILES, 4, HALF], F32, name="table")
@@ -67,56 +68,65 @@ def tile_gemmaattention_pa_kernel(tc, hidden_states, w_qkv_words, w_qkv_scales, 
         nc.gpsimd.iota(position[:], pattern=[[P, TILES]], base=0, channel_multiplier=1)
         make_identity(nc, identity[:])
 
-        fills = [plane_first[:].rearrange("p g n -> p (g n)")] + [plane_rest[:, g, :] for g in range(PASSES)]
-        nc.vector.memset(fills[0].bitcast(I32), 0)
-        nc.vector.tensor_scalar(out=turns[:, :, 1, 0], in0=position[:], scalar1=1.0 / (2.0 * math.pi), scalar2=None,
-                                op0=ALU.mult)
-        for step in range(6):
-            n = 1 << step
-            nc.vector.tensor_scalar(out=turns[:, :, 1, n:2 * n], in0=turns[:, :, 1, 0:n],
-                                    scalar1=THETA ** (-n / HALF), scalar2=None, op0=ALU.mult)
-        nc.vector.tensor_scalar(out=turns[:, :, 0, :], in0=turns[:, :, 1, :], scalar1=0.25, scalar2=None, op0=ALU.add)
-        nc.vector.memset(fills[1].bitcast(I32), 0)
-        nc.vector.tensor_copy(out=whole[:], in_=turns[:])
-        nc.vector.memset(fills[2].bitcast(I32), 0)
-        nc.vector.tensor_tensor(out=frac[:], in0=turns[:], in1=whole[:], op=ALU.subtract)
-        nc.vector.memset(fills[3].bitcast(I32), 0)
-        nc.vector.memset(fills[4].bitcast(I32), 0)
+        nc.vector.memset(planes[0][:].rearrange("p g n -> p (g n)").bitcast(I32), 0)
+        for i in range(RADIX):
+            nc.vector.tensor_scalar(out=turns[:, :, i], in0=position[:], scalar1=THETA ** (-i / HALF) / (2.0 * math.pi),
+                                    scalar2=None, op0=ALU.mult)
+        for i in range(RADIX, HALF, RADIX):
+            nc.vector.tensor_scalar(out=turns[:, :, i:i + RADIX], in0=turns[:, :, 0:RADIX],
+                                    scalar1=THETA ** (-i / HALF), scalar2=None, op0=ALU.mult)
+        nc.vector.tensor_scalar(out=whole[:, :, 0, :], in0=turns[:], scalar1=0.25, scalar2=None, op0=ALU.add)
+        nc.vector.tensor_copy(out=whole[:, :, 1, :], in_=turns[:])
+        nc.vector.scalar_tensor_tensor(out=frac[:, :, 0, :], in0=turns[:], scalar=0.25, in1=whole[:, :, 0, :],
+                                       op0=ALU.add, op1=ALU.subtract)
+        nc.vector.tensor_tensor(out=frac[:, :, 1, :], in0=turns[:], in1=whole[:, :, 1, :], op=ALU.subtract)
+        for plane in planes[1:]:
+            nc.vector.memset(plane[:].rearrange("p g n -> p (g n)").bitcast(I32), 0)
         nc.scalar.activation(out=table[:, :, 0:2, :], in_=frac[:], func=ACT.Sin, scale=2.0 * math.pi)
-        nc.scalar.activation(out=table[:, :, 2, :], in_=frac[:, :, 1, :], func=ACT.Sin, scale=-2.0 * math.pi)
-        nc.vector.tensor_copy(out=table[:, :, 3, :], in_=table[:, :, 0, :])
 
-        for b in range(2):
-            nc.sync.dma_start(out=x_halves[0][b][:], in_=x_hbm[0:P, b * 1024:(b + 1) * 1024])
-        for t in range(1, TILES):
+        def load_scales(index):
+            lo, hi = plane_groups[index]
+            for r in range(4):
+                nc.sync.dma_start(out=planes[index][r:P:32, :, :].bitcast(I32),
+                                  in_=scales_hbm[r, :, :, lo * BLOCK:hi * BLOCK].bitcast(I32))
+
+        def load_words(index):
+            lo, hi = w_groups[index]
+            nc.sync.dma_start(out=w_rest[index][:].bitcast(I32),
+                              in_=words_hbm[:, :, 2 * BLOCK * lo:2 * BLOCK * hi].bitcast(I32))
+
+        def load_tokens(t):
             nc.sync.dma_start(out=x_rest[t - 1][:], in_=x_hbm[t * P:(t + 1) * P, :])
 
-        def load_scales(plane, lo, hi):
-            for r in range(4):
-                nc.sync.dma_start(out=plane[r:P:32, :, :].bitcast(I32), in_=scales_hbm[r, :, :, lo:hi].bitcast(I32))
-
-        load_scales(plane_first, 0, BLOCK)
+        for b in range(2):
+            nc.sync.dma_start(out=x_first[b][:], in_=x_hbm[0:P, b * 1024:(b + 1) * 1024])
+        load_tokens(1)
+        load_tokens(2)
+        load_scales(0)
         for b in range(2):
             nc.sync.dma_start(out=w_first[b][:].bitcast(I32),
                               in_=words_hbm[:, 2 * b:2 * b + 2, 0:2 * BLOCK].bitcast(I32))
-        load_scales(plane_rest, BLOCK, OUT_COLS)
-        for w_tile, (lo, hi) in zip(w_rest, w_groups):
-            nc.sync.dma_start(out=w_tile[:].bitcast(I32),
-                              in_=words_hbm[:, :, 2 * BLOCK * lo:2 * BLOCK * hi].bitcast(I32))
+        load_tokens(3)
+        load_scales(1)
+        load_words(0)
+        load_scales(2)
+        load_words(1)
+        load_words(2)
 
         def weight_operand(j, g, lo, hi):
+            index = [i for i, (a, b) in enumerate(plane_groups) if a <= j < b][0]
+            base = (j - plane_groups[index][0]) * BLOCK
+            w_scales = planes[index][:, g, base + lo:base + hi]
             if j == 0:
-                return w_first[g // 2][:, g % 2, 2 * lo:2 * hi], plane_first[:, g, lo:hi]
+                return w_first[g // 2][:, g % 2, 2 * lo:2 * hi], w_scales
             index = [i for i, (a, b) in enumerate(w_groups) if a <= j < b][0]
             base = (j - w_groups[index][0]) * BLOCK
-            plane_base = (j - 1) * BLOCK
-            return (w_rest[index][:, g, 2 * (base + lo):2 * (base + hi)],
-                    plane_rest[:, g, plane_base + lo:plane_base + hi])
+            return w_rest[index][:, g, 2 * (base + lo):2 * (base + hi)], w_scales
 
-        for t in range(TILES):
+        def quantise_tokens(t):
             for b in range(2):
                 if t == 0:
-                    x_words = x_halves[0][b][:].bitcast(F32)
+                    x_words = x_first[b][:].bitcast(F32)
                 else:
                     x_words = x_rest[t - 1][:, b * 1024:(b + 1) * 1024].bitcast(F32)
                 flipped = psum.tile([P, 2, 2, P], F32, name="flipped", tag="bank")
@@ -156,6 +166,11 @@ def tile_gemmaattention_pa_kernel(tc, hidden_states, w_qkv_words, w_qkv_scales, 
             rows = dest[tiles[0] * P:(tiles[-1] + 1) * P, :].rearrange("(s p) n -> p s n", p=P)
             nc.sync.dma_start(out=rows, in_=rotated[:, 0:count, :, :].rearrange("p s h n -> p s (h n)"))
 
+        quantise_tokens(0)
+        nc.scalar.activation(out=table[:, :, 2, :], in_=frac[:, :, 1, :], func=ACT.Sin, scale=-2.0 * math.pi)
+        nc.vector.tensor_copy(out=table[:, :, 3, :], in_=table[:, :, 0, :])
+        for t in range(1, TILES - 1):
+            quantise_tokens(t)
         late = []
         for j in range(K_BLOCK + 1):
             dest = q_hbm[:, j * BLOCK:(j + 1) * BLOCK] if j < Q_BLOCKS else k_hbm
@@ -170,6 +185,8 @@ def tile_gemmaattention_pa_kernel(tc, hidden_states, w_qkv_words, w_qkv_scales, 
                 for s, t in enumerate(tiles):
                     acc = project(t, j, 0, BLOCK)
                     rotate_products(t, acc, products[:, s, :, :, :])
+                    if j == 0 and t == 0:
+                        quantise_tokens(TILES - 1)
                 if j == K_BLOCK and tiles[0] >= 1:
                     late.append((products, dest, tiles))
                 else:

@@ -65,6 +65,16 @@ def tile_gemmaattention_pa_kernel(tc, hidden_states, w_qkv_words, w_qkv_scales, 
         frac = keep.tile([P, TILES, 2, HALF], F32, name="frac")
         table = keep.tile([P, TILES, 4, HALF], F32, name="table")
 
+        zeros = keep.tile([P, BLOCK], BF16, name="zeros")
+        unread = psum.tile([P, BLOCK], F32, name="unread", tag="bank")
+
+        def warm_up(count):
+            for rep in range(count):
+                nc.tensor.matmul(out=unread[:], lhsT=zeros[:, 0:P], rhs=zeros[:], start=True, stop=True)
+
+        nc.vector.memset(zeros[:], 0.0)
+        warm_up(4)
+
         nc.gpsimd.iota(position[:], pattern=[[P, TILES]], base=0, channel_multiplier=1)
         make_identity(nc, identity[:])
 
@@ -167,10 +177,12 @@ def tile_gemmaattention_pa_kernel(tc, hidden_states, w_qkv_words, w_qkv_scales, 
             nc.sync.dma_start(out=rows, in_=rotated[:, 0:count, :, :].rearrange("p s h n -> p s (h n)"))
 
         quantise_tokens(0)
+        warm_up(2)
         nc.scalar.activation(out=table[:, :, 2, :], in_=frac[:, :, 1, :], func=ACT.Sin, scale=-2.0 * math.pi)
         nc.vector.tensor_copy(out=table[:, :, 3, :], in_=table[:, :, 0, :])
         for t in range(1, TILES - 1):
             quantise_tokens(t)
+        warm_up(2)
         late = []
         for j in range(K_BLOCK + 1):
             dest = q_hbm[:, j * BLOCK:(j + 1) * BLOCK] if j < Q_BLOCKS else k_hbm

@@ -78,21 +78,24 @@ def tile_gemmaattention_pa_kernel(tc, hidden_states, w_qkv_words, w_qkv_scales, 
         nc.gpsimd.iota(position[:], pattern=[[P, TILES]], base=0, channel_multiplier=1)
         make_identity(nc, identity[:])
 
-        nc.vector.memset(planes[0][:].rearrange("p g n -> p (g n)").bitcast(I32), 0)
+        def fill_plane(index):
+            nc.vector.memset(planes[index][:].rearrange("p g n -> p (g n)").bitcast(I32), 0)
+
         for i in range(RADIX):
             nc.vector.tensor_scalar(out=turns[:, :, i], in0=position[:], scalar1=THETA ** (-i / HALF) / (2.0 * math.pi),
                                     scalar2=None, op0=ALU.mult)
         for i in range(RADIX, HALF, RADIX):
             nc.vector.tensor_scalar(out=turns[:, :, i:i + RADIX], in0=turns[:, :, 0:RADIX],
                                     scalar1=THETA ** (-i / HALF), scalar2=None, op0=ALU.mult)
+        fill_plane(0)
         nc.vector.tensor_scalar(out=whole[:, :, 0, :], in0=turns[:], scalar1=0.25, scalar2=None, op0=ALU.add)
         nc.vector.tensor_copy(out=whole[:, :, 1, :], in_=turns[:])
+        fill_plane(1)
         nc.vector.scalar_tensor_tensor(out=frac[:, :, 0, :], in0=turns[:], scalar=0.25, in1=whole[:, :, 0, :],
                                        op0=ALU.add, op1=ALU.subtract)
         nc.vector.tensor_tensor(out=frac[:, :, 1, :], in0=turns[:], in1=whole[:, :, 1, :], op=ALU.subtract)
-        for plane in planes[1:]:
-            nc.vector.memset(plane[:].rearrange("p g n -> p (g n)").bitcast(I32), 0)
-        nc.scalar.activation(out=table[:, :, 0:2, :], in_=frac[:], func=ACT.Sin, scale=2.0 * math.pi)
+        fill_plane(2)
+        nc.scalar.activation(out=table[:, 0, 0:2, :], in_=frac[:, 0, :, :], func=ACT.Sin, scale=2.0 * math.pi)
 
         def load_scales(index):
             lo, hi = plane_groups[index]
@@ -111,14 +114,14 @@ def tile_gemmaattention_pa_kernel(tc, hidden_states, w_qkv_words, w_qkv_scales, 
         for b in range(2):
             nc.sync.dma_start(out=x_first[b][:], in_=x_hbm[0:P, b * 1024:(b + 1) * 1024])
         load_tokens(1)
-        load_tokens(2)
         load_scales(0)
         for b in range(2):
             nc.sync.dma_start(out=w_first[b][:].bitcast(I32),
                               in_=words_hbm[:, 2 * b:2 * b + 2, 0:2 * BLOCK].bitcast(I32))
-        load_tokens(3)
+        load_tokens(2)
         load_scales(1)
         load_words(0)
+        load_tokens(3)
         load_scales(2)
         load_words(1)
         load_words(2)
@@ -167,42 +170,45 @@ def tile_gemmaattention_pa_kernel(tc, hidden_states, w_qkv_words, w_qkv_scales, 
                 in1=table[:, t:t + 1, :, :].rearrange("p one q i -> p one (q i)").to_broadcast([P, HEADS_PER_BLOCK, 4 * HALF]),
                 op=ALU.mult)
 
-        def add_and_store(engine, products, dest, tiles):
-            count = len(tiles)
+        def add_and_store(engine, products, t, blocks):
+            count = len(blocks)
             rotated = work.tile([P, 2, HEADS_PER_BLOCK, HEAD], F32, name="rotated", bufs=6)
             engine.tensor_tensor(out=rotated[:, 0:count, :, :].rearrange("p s h n -> p (s h) n"),
                                  in0=products[:, 0:count, :, 0, :].rearrange("p s h n -> p (s h) n"),
                                  in1=products[:, 0:count, :, 1, :].rearrange("p s h n -> p (s h) n"), op=ALU.add)
-            rows = dest[tiles[0] * P:(tiles[-1] + 1) * P, :].rearrange("(s p) n -> p s n", p=P)
-            nc.sync.dma_start(out=rows, in_=rotated[:, 0:count, :, :].rearrange("p s h n -> p s (h n)"))
+            if blocks[0] == K_BLOCK:
+                dest = k_hbm[t * P:(t + 1) * P, :]
+            else:
+                dest = q_hbm[t * P:(t + 1) * P, blocks[0] * BLOCK:(blocks[-1] + 1) * BLOCK]
+            nc.sync.dma_start(out=dest, in_=rotated[:, 0:count, :, :].rearrange("p s h n -> p (s h n)"))
+
+        def multiply(t, blocks):
+            products = work.tile([P, 2, HEADS_PER_BLOCK, 2, HEAD], F32, name="products", bufs=4)
+            for s, j in enumerate(blocks):
+                rotate_products(t, project(t, j, 0, BLOCK), products[:, s, :, :, :])
+            return products
+
+        def rotate(t, blocks):
+            add_and_store(nc.gpsimd, multiply(t, blocks), t, blocks)
 
         quantise_tokens(0)
         warm_up(2)
+        quantise_tokens(1)
         nc.scalar.activation(out=table[:, :, 2, :], in_=frac[:, :, 1, :], func=ACT.Sin, scale=-2.0 * math.pi)
+        nc.scalar.activation(out=table[:, 1:TILES, 0:2, :], in_=frac[:, 1:TILES, :, :], func=ACT.Sin,
+                             scale=2.0 * math.pi)
         nc.vector.tensor_copy(out=table[:, :, 3, :], in_=table[:, :, 0, :])
-        for t in range(1, TILES - 1):
-            quantise_tokens(t)
-        warm_up(2)
-        late = []
-        for j in range(K_BLOCK + 1):
-            dest = q_hbm[:, j * BLOCK:(j + 1) * BLOCK] if j < Q_BLOCKS else k_hbm
-            if j == 0:
-                groups = [[0], [1], [2, 3]]
-            elif j == K_BLOCK:
-                groups = [[0], [1], [2], [3]]
-            else:
-                groups = [[0, 1], [2, 3]]
-            for tiles in groups:
-                products = work.tile([P, 2, HEADS_PER_BLOCK, 2, HEAD], F32, name="products", bufs=4)
-                for s, t in enumerate(tiles):
-                    acc = project(t, j, 0, BLOCK)
-                    rotate_products(t, acc, products[:, s, :, :, :])
-                    if j == 0 and t == 0:
-                        quantise_tokens(TILES - 1)
-                if j == K_BLOCK and tiles[0] >= 1:
-                    late.append((products, dest, tiles))
-                else:
-                    add_and_store(nc.gpsimd, products, dest, tiles)
+        for j in range(2):
+            for t in range(2):
+                rotate(t, [j])
+            quantise_tokens(2 + j)
+        rotate(2, [0])
+        rotate(2, [1])
+        rotate(3, [0, 1])
+        for t in range(TILES):
+            rotate(t, [2, 3])
+        rotate(0, [K_BLOCK])
+        late = [(multiply(t, [K_BLOCK]), t, [K_BLOCK]) for t in range(1, TILES)]
 
         def store_values(t, lo, hi):
             acc = project(t, V_BLOCK, lo, hi)
@@ -217,4 +223,7 @@ def tile_gemmaattention_pa_kernel(tc, hidden_states, w_qkv_words, w_qkv_scales, 
         add_and_store(nc.vector, *late[2])
         store_values(2, 0, BLOCK)
         store_values(3, 0, BLOCK // 2)
-        store_values(3, BLOCK // 2, BLOCK)
+        acc = project(3, V_BLOCK, BLOCK // 2, BLOCK)
+        last = work.tile([P, BLOCK // 2], F32, name="last", bufs=1)
+        nc.vector.tensor_copy(out=last[:], in_=acc[:, 0:BLOCK // 2])
+        nc.sync.dma_start(out=v_hbm[3 * P:4 * P, BLOCK // 2:BLOCK], in_=last[:])

import math
from contextlib import ExitStack

import concourse.mybir as mybir
from concourse.masks import make_identity

F32 = mybir.dt.float32
BF16 = mybir.dt.bfloat16
I32 = mybir.dt.int32
U32 = mybir.dt.uint32
U8 = mybir.dt.uint8
E5M2X4 = mybir.dt.float8_e5m2_x4
E2M1X4 = mybir.dt.float4_e2m1fn_x4
ALU = mybir.AluOpType
ACT = mybir.ActivationFunctionType

P = 128
TOKENS, HIDDEN, OUT_COLS = 512, 2048, 3072
HEAD, HALF = 128, 64
THETA = 10000.0
PASSES = HIDDEN // 512
TILES = TOKENS // P
BLOCK = 512
BLOCKS = OUT_COLS // BLOCK
HEADS_PER_BLOCK = BLOCK // HEAD
Q_BLOCKS = 4
K_BLOCK, V_BLOCK = 4, 5
RADIX = 8

FLOPS = 2 * TOKENS * HIDDEN * OUT_COLS


def tile_gemmaattention_pa_kernel(tc, hidden_states, w_qkv_words, w_qkv_scales, out_0, out_1, out_2):
    nc = tc.nc
    x_hbm = hidden_states.rearrange("b s k -> (b s) k")
    q_hbm = out_0.rearrange("b s h d -> (b s) (h d)")
    k_hbm = out_1.rearrange("b s h d -> (b s) (h d)")
    v_hbm = out_2.rearrange("b s h d -> (b s) (h d)")
    words_hbm = w_qkv_words.rearrange("g p c -> p g c")
    scales_hbm = w_qkv_scales.rearrange("g (quad r) n -> r quad g n", r=4)

    with ExitStack() as ctx:
        keep = ctx.enter_context(tc.tile_pool(name="keep", bufs=1))
        work = ctx.enter_context(tc.tile_pool(name="work", bufs=3))
        psum = ctx.enter_context(tc.psum_pool(name="psum", bufs=8))
        ctx.enter_context(tc.manual_schedule())

        x_first = [keep.tile([P, HIDDEN // 2], BF16, name="x_0_%d" % b, align_bytes=64) for b in range(2)]
        x_rest = [keep.tile([P, HIDDEN], BF16, name="x_%d" % t, align_bytes=64) for t in range(1, TILES)]
        codes = [[keep.tile([P, 2, P], U32, name="codes_%d_%d" % (t, b), align_bytes=64) for b in range(2)]
                 for t in range(TILES)]
        x_scales = [[keep.tile([P, 2, P], U8, name="xscales_%d_%d" % (t, b), align_bytes=64) for b in range(2)]
                    for t in range(TILES)]
        plane_groups = [(0, 1), (1, 2), (2, 6)]
        planes = [keep.tile([P, PASSES, BLOCK * (hi - lo)], U8, name="plane_%d" % lo, align_bytes=64)
                  for lo, hi in plane_groups]
        w_first = [keep.tile([P, 2, 2 * BLOCK], U8, name="w_first_%d" % b, align_bytes=64) for b in range(2)]
        w_groups = [(1, 2), (2, 4), (4, 6)]
        w_rest = [keep.tile([P, PASSES, 2 * BLOCK * (hi - lo)], U8, name="w_%d" % lo, align_bytes=64)
                  for lo, hi in w_groups]
        identity = keep.tile([P, P], F32, name="identity")
        position = keep.tile([P, TILES], I32, name="position")
        turns = keep.tile([P, TILES, HALF], F32, name="turns")
        whole = keep.tile([P, TILES, 2, HALF], I32, name="whole")
        frac = keep.tile([P, TILES, 2, HALF], F32, name="frac")
        table = keep.tile([P, TILES, 4, HALF], F32, name="table")

        zeros = keep.tile([P, BLOCK], BF16, name="zeros")
        unread = psum.tile([P, BLOCK], F32, name="unread", tag="bank")

        def warm_up(count):
            for rep in range(count):
                nc.tensor.matmul(out=unread[:], lhsT=zeros[:, 0:P], rhs=zeros[:], start=True, stop=True)

        nc.vector.memset(zeros[:], 0.0)
        warm_up(4)

        nc.gpsimd.iota(position[:], pattern=[[P, TILES]], base=0, channel_multiplier=1)
        make_identity(nc, identity[:])

        def fill_plane(index):
            nc.vector.memset(planes[index][:].rearrange("p g n -> p (g n)").bitcast(I32), 0)

        for i in range(RADIX):
            nc.vector.tensor_scalar(out=turns[:, :, i], in0=position[:], scalar1=THETA ** (-i / HALF) / (2.0 * math.pi),
                                    scalar2=None, op0=ALU.mult)
        for i in range(RADIX, HALF, RADIX):
            nc.vector.tensor_scalar(out=turns[:, :, i:i + RADIX], in0=turns[:, :, 0:RADIX],
                                    scalar1=THETA ** (-i / HALF), scalar2=None, op0=ALU.mult)
        fill_plane(0)
        nc.vector.tensor_scalar(out=whole[:, :, 0, :], in0=turns[:], scalar1=0.25, scalar2=None, op0=ALU.add)
        nc.vector.tensor_copy(out=whole[:, :, 1, :], in_=turns[:])
        fill_plane(1)
        nc.vector.scalar_tensor_tensor(out=frac[:, :, 0, :], in0=turns[:], scalar=0.25, in1=whole[:, :, 0, :],
                                       op0=ALU.add, op1=ALU.subtract)
        nc.vector.tensor_tensor(out=frac[:, :, 1, :], in0=turns[:], in1=whole[:, :, 1, :], op=ALU.subtract)
        fill_plane(2)
        nc.scalar.activation(out=table[:, 0, 0:2, :], in_=frac[:, 0, :, :], func=ACT.Sin, scale=2.0 * math.pi)

        def load_scales(index):
            lo, hi = plane_groups[index]
            for r in range(4):
                nc.sync.dma_start(out=planes[index][r:P:32, :, :].bitcast(I32),
                                  in_=scales_hbm[r, :, :, lo * BLOCK:hi * BLOCK].bitcast(I32))

        def load_words(index):
            lo, hi = w_groups[index]
            nc.sync.dma_start(out=w_rest[index][:].bitcast(I32),
                              in_=words_hbm[:, :, 2 * BLOCK * lo:2 * BLOCK * hi].bitcast(I32))

        def load_tokens(t):
            nc.sync.dma_start(out=x_rest[t - 1][:], in_=x_hbm[t * P:(t + 1) * P, :])

        for b in range(2):
            nc.sync.dma_start(out=x_first[b][:], in_=x_hbm[0:P, b * 1024:(b + 1) * 1024])
        load_tokens(1)
        load_scales(0)
        for b in range(2):
            nc.sync.dma_start(out=w_first[b][:].bitcast(I32),
                              in_=words_hbm[:, 2 * b:2 * b + 2, 0:2 * BLOCK].bitcast(I32))
        load_tokens(2)
        load_scales(1)
        load_words(0)
        load_tokens(3)
        load_scales(2)
        load_words(1)
        load_words(2)

        def weight_operand(j, g, lo, hi):
            index = [i for i, (a, b) in enumerate(plane_groups) if a <= j < b][0]
            base = (j - plane_groups[index][0]) * BLOCK
            w_scales = planes[index][:, g, base + lo:base + hi]
            if j == 0:
                return w_first[g // 2][:, g % 2, 2 * lo:2 * hi], w_scales
            index = [i for i, (a, b) in enumerate(w_groups) if a <= j < b][0]
            base = (j - w_groups[index][0]) * BLOCK
            return w_rest[index][:, g, 2 * (base + lo):2 * (base + hi)], w_scales

        def quantise_tokens(t):
            for b in range(2):
                if t == 0:
                    x_words = x_first[b][:].bitcast(F32)
                else:
                    x_words = x_rest[t - 1][:, b * 1024:(b + 1) * 1024].bitcast(F32)
                flipped = psum.tile([P, 2, 2, P], F32, name="flipped", tag="bank")
                for g in range(2):
                    for u in range(2):
                        nc.tensor.transpose(flipped[:, g, u, :], x_words[:, 256 * g + u:256 * (g + 1):2], identity[:])
                grouped = work.tile([P, 2, P, 2], F32, name="grouped", align_bytes=64)
                nc.scalar.copy(out=grouped[:], in_=flipped[:].rearrange("p g u r -> p g r u"))
                nc.vector.quantize_mx(out=codes[t][b][:].rearrange("p g r -> p (g r)").bitcast(E5M2X4),
                                      scales=x_scales[t][b][:].rearrange("p g r -> p (g r)"),
                                      in_=grouped[:].rearrange("p g r u -> p (g r u)").bitcast(BF16))

        def project(t, j, lo, hi):
            acc = psum.tile([P, BLOCK], F32, name="acc", tag="bank")
            for g in range(PASSES):
                w_words, w_scales = weight_operand(j, g, lo, hi)
                nc.tensor.matmul_mx(out=acc[:, 0:hi - lo], lhsT=codes[t][g // 2][:, g % 2, :].bitcast(E5M2X4),
                                    lhsT_scale=x_scales[t][g // 2][:, g % 2, :],
                                    rhs=w_words.bitcast(E2M1X4), rhs_scale=w_scales,
                                    start=(g == 0), stop=(g == PASSES - 1))
            return acc

        def rotate_products(t, acc, products):
            halves = acc[:].rearrange("p (hh one i) -> p hh one i", one=1, i=HALF)
            nc.vector.tensor_tensor(
                out=products.rearrange("p h src n -> p (h src n)").rearrange("p (hh dst i) -> p hh dst i", dst=2, i=HALF),
                in0=halves.to_broadcast([P, 2 * HEADS_PER_BLOCK, 2, HALF]),
                in1=table[:, t:t + 1, :, :].rearrange("p one q i -> p one (q i)").to_broadcast([P, HEADS_PER_BLOCK, 4 * HALF]),
                op=ALU.mult)

        def add_and_store(engine, products, t, blocks):
            count = len(blocks)
            rotated = work.tile([P, 2, HEADS_PER_BLOCK, HEAD], F32, name="rotated", bufs=6)
            engine.tensor_tensor(out=rotated[:, 0:count, :, :].rearrange("p s h n -> p (s h) n"),
                                 in0=products[:, 0:count, :, 0, :].rearrange("p s h n -> p (s h) n"),
                                 in1=products[:, 0:count, :, 1, :].rearrange("p s h n -> p (s h) n"), op=ALU.add)
            if blocks[0] == K_BLOCK:
                dest = k_hbm[t * P:(t + 1) * P, :]
            else:
                dest = q_hbm[t * P:(t + 1) * P, blocks[0] * BLOCK:(blocks[-1] + 1) * BLOCK]
            nc.sync.dma_start(out=dest, in_=rotated[:, 0:count, :, :].rearrange("p s h n -> p (s h n)"))

        def multiply(t, blocks):
            products = work.tile([P, 2, HEADS_PER_BLOCK, 2, HEAD], F32, name="products", bufs=4)
            for s, j in enumerate(blocks):
                rotate_products(t, project(t, j, 0, BLOCK), products[:, s, :, :, :])
            return products

        def rotate(t, blocks):
            add_and_store(nc.gpsimd, multiply(t, blocks), t, blocks)

        quantise_tokens(0)
        warm_up(2)
        quantise_tokens(1)
        nc.scalar.activation(out=table[:, :, 2, :], in_=frac[:, :, 1, :], func=ACT.Sin, scale=-2.0 * math.pi)
        nc.scalar.activation(out=table[:, 1:TILES, 0:2, :], in_=frac[:, 1:TILES, :, :], func=ACT.Sin,
                             scale=2.0 * math.pi)
        nc.vector.tensor_copy(out=table[:, :, 3, :], in_=table[:, :, 0, :])
        for j in range(2):
            for t in range(2):
                rotate(t, [j])
            quantise_tokens(2 + j)
        rotate(2, [0])
        rotate(2, [1])
        rotate(3, [0, 1])
        for t in range(TILES):
            rotate(t, [2, 3])
        rotate(0, [K_BLOCK])
        late = [(multiply(t, [K_BLOCK]), t, [K_BLOCK]) for t in range(1, TILES)]

        def store_values(t, lo, hi):
            acc = project(t, V_BLOCK, lo, hi)
            values = work.tile([P, BLOCK], F32, name="values", bufs=5)
            nc.scalar.copy(out=values[:, 0:hi - lo], in_=acc[:, 0:hi - lo])
            nc.scalar.dma_start(out=v_hbm[t * P:(t + 1) * P, lo:hi], in_=values[:, 0:hi - lo])

        store_values(0, 0, BLOCK)
        add_and_store(nc.vector, *late[0])
        store_values(1, 0, BLOCK)
        add_and_store(nc.vector, *late[1])
        add_and_store(nc.vector, *late[2])
        store_values(2, 0, BLOCK)
        store_values(3, 0, BLOCK // 2)
        acc = project(3, V_BLOCK, BLOCK // 2, BLOCK)
        last = work.tile([P, BLOCK // 2], F32, name="last", bufs=1)
        nc.vector.tensor_copy(out=last[:], in_=acc[:, 0:BLOCK // 2])
        nc.sync.dma_start(out=v_hbm[3 * P:4 * P, BLOCK // 2:BLOCK], in_=last[:])
